import numpy as np
import ml_dtypes

BF16 = ml_dtypes.bfloat16


def bf(x):
    return np.asarray(x, np.float32).astype(BF16)


def f32(x):
    return np.asarray(x, np.float32)


def f64(x):
    return np.asarray(x).astype(np.float64)


def striped(idx):
    return np.tile(idx.reshape(-1, 16).T, (8, 1))


C, S, N, F, K, D = 1024, 2048, 1024, 1024, 4, 256
DENS, SLOPE = 0.0625, 0.2


def setup_inputs():
    return {
        "adj": f32(np.random.random((C, S)) < DENS),
        "ht": bf(np.random.standard_normal((F, N))),
        "w": bf(np.sqrt(2.0 / (F + D)) * np.random.standard_normal((F, K * D))),
        "a_src": f32(0.8 / np.sqrt(D) * np.random.standard_normal((K * D, 1))),
        "a_dst": f32(0.8 / np.sqrt(D) * np.random.standard_normal((K * D, 1))),
        "b": f32(0.1 * np.random.standard_normal((K * D, 1))),
        "offs": striped(np.random.permutation(S)[:N]),
    }


def reference(adj, ht, w, a_src, a_dst, b, offs):
    idx = offs[:16].T.reshape(-1)
    hw = f64(ht).T @ f64(w)
    mask = f64(adj)[:, idx]
    res = np.zeros((C, K * D))
    for k in range(K):
        sl = slice(k * D, (k + 1) * D)
        s1 = hw[:, sl] @ f64(a_src)[sl]
        s2 = hw[:, sl] @ f64(a_dst)[sl]
        v = s1 + s2.T
        e = np.exp(np.maximum(v, SLOPE * v))
        p = mask * e
        r = (p @ hw[:, sl]) / p.sum(axis=1, keepdims=True) + f64(b)[sl].T
        res[:, sl] = np.maximum(r, 0.0) + np.exp(np.minimum(r, 0.0)) - 1.0
    return res

@@ -1,0 +1,179 @@
+import concourse.mybir as mybir
+from concourse.masks import make_identity
+
+P = 128
+NODES = 1024
+GRAPH = 2048
+FEATS = 1024
+HEADS = 4
+DH = 256
+NB = NODES // P
+FB = FEATS // P
+QB = HEADS * DH // P
+HALF = 512
+ROW = DH + 2
+
+FLOPS = 2 * FEATS * NODES * HEADS * DH + 2 * HEADS * NODES * NODES * DH
+
+F32 = mybir.dt.float32
+BF16 = mybir.dt.bfloat16
+U16 = mybir.dt.uint16
+ALU = mybir.AluOpType
+ACT = mybir.ActivationFunctionType
+
+
+def tile_graphattentionlayer_b_kernel(tc, adj, ht, w, a_src, a_dst, b, offs, out):
+    nc = tc.nc
+    with (
+        tc.tile_pool(name="lists", bufs=1) as lists,
+        tc.tile_pool(name="held", bufs=1) as held,
+        tc.tile_pool(name="e_pool", bufs=2) as e_pool,
+        tc.tile_pool(name="p_pool", bufs=3) as p_pool,
+        tc.tile_pool(name="pb_pool", bufs=8) as pb_pool,
+        tc.tile_pool(name="pt_pool", bufs=3) as pt_pool,
+        tc.tile_pool(name="tail", bufs=3) as tail,
+        tc.psum_pool(name="ps_flip", bufs=2) as ps_flip,
+        tc.psum_pool(name="ps_small", bufs=1) as ps_small,
+        tc.psum_pool(name="ps_wide", bufs=3) as ps_wide,
+        tc.psum_pool(name="ps_acc", bufs=2) as ps_acc,
+    ):
+        offsets = lists.tile([P, NODES // 16], U16, name="offsets")
+        nc.sync.dma_start(offsets[:], offs)
+
+        a_src_sb = held.tile([P, QB], F32, name="a_src_sb")
+        a_dst_sb = held.tile([P, QB], F32, name="a_dst_sb")
+        b_row = held.tile([1, HEADS * DH], F32, name="b_row")
+        nc.scalar.dma_start(a_src_sb[:], a_src.rearrange("(a p) o -> p (a o)", p=P))
+        nc.scalar.dma_start(a_dst_sb[:], a_dst.rearrange("(a p) o -> p (a o)", p=P))
+        nc.scalar.dma_start(b_row[:], b.rearrange("q o -> o q"))
+
+        w_sb = held.tile([P, FB, HEADS * DH], BF16, name="w_sb")
+        ht_sb = held.tile([P, FB, NODES], BF16, name="ht_sb")
+        w_view = w.rearrange("(p a) q -> p a q", a=FB)
+        ht_view = ht.rearrange("(p a) n -> p a n", a=FB)
+        for a in range(0, FB, 2):
+            queue = nc.sync if a % 4 == 0 else nc.scalar
+            queue.dma_start(w_sb[:, a : a + 2, :], w_view[:, a : a + 2, :])
+        for a in range(0, FB, 2):
+            queue = nc.sync if a % 4 == 0 else nc.scalar
+            queue.dma_start(ht_sb[:, a : a + 2, :], ht_view[:, a : a + 2, :])
+        adj_sb = [held.tile([P, GRAPH], F32, name="adj%d" % ib) for ib in range(NB)]
+        for ib in range(NB):
+            queue = nc.sync if ib % 2 == 0 else nc.scalar
+            queue.dma_start(adj_sb[ib][:], adj[ib * P : (ib + 1) * P, :])
+
+        ident_bf = held.tile([P, P], BF16, name="ident_bf")
+        ident_f32 = held.tile([P, P], F32, name="ident_f32")
+        make_identity(nc, ident_bf[:])
+        make_identity(nc, ident_f32[:])
+        ones_bf = held.tile([P, P], BF16, name="ones_bf")
+        nc.vector.memset(ones_bf[:], 1.0)
+        b_bf = held.tile([P, HEADS * DH], BF16, name="b_bf")
+        nc.gpsimd.memset(b_bf[:], 0.0)
+        nc.vector.tensor_copy(b_bf[0:1, :], b_row[:])
+        a_bf = held.tile([P, QB, 2], BF16, name="a_bf")
+        nc.vector.tensor_copy(a_bf[:, :, 0:1], a_src_sb[:].unsqueeze(2))
+        nc.vector.tensor_copy(a_bf[:, :, 1:2], a_dst_sb[:].unsqueeze(2))
+
+        wa_ps = ps_small.tile([P, FB, 2 * HEADS], F32, tag="small", name="wa_ps")
+        for a in range(FB):
+            wt_ps = ps_flip.tile([P, QB, P], BF16, tag="flip", name="wt_ps")
+            for qb in range(QB):
+                nc.tensor.transpose(wt_ps[:, qb, :], w_sb[:, a, qb * P : (qb + 1) * P], ident_bf[:])
+            wt_sb = pt_pool.tile([P, QB, P], BF16, tag="flipped", name="wt_sb")
+            nc.vector.tensor_copy(wt_sb[:], wt_ps[:])
+            for qb in range(QB):
+                k = qb // 2
+                nc.tensor.matmul(
+                    wa_ps[:, a, 2 * k : 2 * k + 2], lhsT=wt_sb[:, qb, :], rhs=a_bf[:, qb, :],
+                    start=(qb % 2 == 0), stop=(qb % 2 == 1),
+                )
+        wa_bf = held.tile([P, FB, 2 * HEADS], BF16, name="wa_bf")
+        nc.vector.tensor_copy(wa_bf[:], wa_ps[:])
+
+        s_ps = ps_small.tile([P, NB, 2 * HEADS], F32, tag="small", name="s_ps")
+        for nb in range(NB):
+            for a in range(FB):
+                nc.tensor.matmul(
+                    s_ps[:, nb, :], lhsT=ht_sb[:, a, nb * P : (nb + 1) * P], rhs=wa_bf[:, a, :],
+                    start=(a == 0), stop=(a == FB - 1),
+                )
+        s_view = s_ps[:].rearrange("p n (k t) -> p n k t", t=2)
+        h1 = held.tile([P, NB, HEADS], F32, name="h1")
+        g2 = held.tile([P, NB, HEADS], F32, name="g2")
+        h2_col = held.tile([P, NB, HEADS], F32, name="h2_col")
+        nc.scalar.activation(h2_col[:], s_view[:, :, :, 1], ACT.Exp, scale=0.8)
+        nc.scalar.activation(h1[:], s_view[:, :, :, 0], ACT.Exp, scale=0.8)
+        nc.scalar.activation(g2[:], s_view[:, :, :, 1], ACT.Exp, scale=0.2)
+
+        h2 = held.tile([P, HEADS, NODES], F32, name="h2")
+        hwx = held.tile([P, NB, HEADS, ROW], BF16, name="hwx")
+        nc.scalar.copy(hwx[:, :, :, DH : DH + 1], g2[:].unsqueeze(3))
+
+        def spread_h2(k):
+            for half in range(NODES // HALF):
+                spread_ps = ps_wide.tile([P, HALF], F32, tag="wide", name="spread_ps")
+                for c in range(HALF // P):
+                    nb = half * (HALF // P) + c
+                    nc.tensor.matmul(
+                        spread_ps[:, c * P : (c + 1) * P],
+                        lhsT=h2_col[:, nb, k : k + 1].to_broadcast([P, P]), rhs=ident_f32[:],
+                        start=True, stop=True,
+                    )
+                nc.vector.tensor_copy(h2[:, k, half * HALF : (half + 1) * HALF], spread_ps[:])
+
+        def project(pair):
+            cols = slice(pair * HALF, (pair + 1) * HALF)
+            for nb in range(NB):
+                hw_ps = ps_wide.tile([P, HALF], F32, tag="wide", name="hw_ps")
+                for a in range(FB):
+                    nc.tensor.matmul(
+                        hw_ps[:], lhsT=ht_sb[:, a, nb * P : (nb + 1) * P], rhs=w_sb[:, a, cols],
+                        start=(a == 0), stop=False,
+                    )
+                nc.tensor.matmul(hw_ps[:], lhsT=ones_bf[:], rhs=b_bf[:, cols], start=False, stop=True)
+                for kk in range(2):
+                    k = 2 * pair + kk
+                    nc.scalar.activation(
+                        hwx[:, nb, k, 0:DH], hw_ps[:, kk * DH : (kk + 1) * DH], ACT.Copy,
+                        scale=g2[:, nb, k : k + 1],
+                    )
+
+        def attend(ib, k, result):
+            e = e_pool.tile([P, NODES], F32, name="e")
+            nc.vector.tensor_scalar(
+                e[:], h2[:, k, :], h1[:, ib, k : k + 1], 1.0, op0=ALU.mult, op1=ALU.max
+            )
+            p = p_pool.tile([P, NODES], F32, name="p")
+            nc.vector.tensor_tensor(p[:], adj_sb[ib][:].indirect(offsets[:]), e[:], ALU.mult)
+            p_bf = pb_pool.tile([P, NODES], BF16, name="p_bf")
+            nc.scalar.copy(p_bf[:], p[:])
+            pt_ps = ps_flip.tile([P, NB, P], BF16, tag="flip", name="pt_ps")
+            for jb in range(NB):
+                nc.tensor.transpose(pt_ps[:, jb, :], p_bf[:, jb * P : (jb + 1) * P], ident_bf[:])
+            pt = pt_pool.tile([P, NB, P], BF16, tag="flipped", name="pt")
+            nc.scalar.copy(pt[:], pt_ps[:])
+            acc = ps_acc.tile([P, DH + 1], F32, name="acc")
+            for jb in range(NB):
+                nc.tensor.matmul(
+                    acc[:], lhsT=pt[:, jb, :], rhs=hwx[:, jb, k, 0 : DH + 1],
+                    start=(jb == 0), stop=(jb == NB - 1),
+                )
+            inv = tail.tile([P, 1], F32, name="inv")
+            nc.vector.reciprocal(inv[:], acc[:, DH : DH + 1])
+            ex = tail.tile([P, DH], F32, name="ex")
+            nc.scalar.activation(ex[:], acc[:, 0:DH], ACT.Exp, scale=inv[:])
+            nc.vector.tensor_scalar(ex[:], ex[:], 1.0, -1.0, op0=ALU.min, op1=ALU.add)
+            nc.vector.scalar_tensor_tensor(
+                result, in0=acc[:, 0:DH], scalar=inv[:], in1=ex[:], op0=ALU.mult, op1=ALU.max
+            )
+
+        for pair in range(HEADS // 2):
+            spread_h2(2 * pair)
+            spread_h2(2 * pair + 1)
+            project(pair)
+            for ib in range(NB):
+                o = tail.tile([P, HALF], F32, name="o")
+                for kk in range(2):
+                    attend(ib, 2 * pair + kk, o[:, kk * DH : (kk + 1) * DH])
+                nc.sync.dma_start(out[ib * P : (ib + 1) * P, pair * HALF : (pair + 1) * HALF], o[:])

@@ -10,8 +10,16 @@ DH = 256
 NB = NODES // P
 FB = FEATS // P
 QB = HEADS * DH // P
-HALF = 512
+BANK = 512
 ROW = DH + 2
+UNITS = HEADS * NB
+TERMS = 3
+
+ROUND_LAG = 1
+FLIP_LAG = 2
+WEIGH_LAG = 3
+EXP_LAG = 4
+ELU_LAG = 5
 
 FLOPS = 2 * FEATS * NODES * HEADS * DH + 2 * HEADS * NODES * NODES * DH
 
@@ -28,14 +36,11 @@ def tile_graphattentionlayer_b_kernel(tc, adj, ht, w, a_src, a_dst, b, offs, out
         tc.tile_pool(name="lists", bufs=1) as lists,
         tc.tile_pool(name="held", bufs=1) as held,
         tc.tile_pool(name="e_pool", bufs=2) as e_pool,
-        tc.tile_pool(name="p_pool", bufs=3) as p_pool,
-        tc.tile_pool(name="pb_pool", bufs=8) as pb_pool,
-        tc.tile_pool(name="pt_pool", bufs=3) as pt_pool,
-        tc.tile_pool(name="tail", bufs=3) as tail,
-        tc.psum_pool(name="ps_flip", bufs=2) as ps_flip,
-        tc.psum_pool(name="ps_small", bufs=1) as ps_small,
-        tc.psum_pool(name="ps_wide", bufs=3) as ps_wide,
-        tc.psum_pool(name="ps_acc", bufs=2) as ps_acc,
+        tc.tile_pool(name="ring", bufs=3) as ring,
+        tc.tile_pool(name="tail", bufs=4) as tail,
+        tc.psum_pool(name="ps_flip", bufs=3) as ps_flip,
+        tc.psum_pool(name="ps_acc", bufs=ELU_LAG - WEIGH_LAG + 1) as ps_acc,
+        tc.psum_pool(name="ps_wide", bufs=2) as ps_wide,
     ):
         offsets = lists.tile([P, NODES // 16], U16, name="offsets")
         nc.sync.dma_start(offsets[:], offs)
@@ -59,13 +64,10 @@ def tile_graphattentionlayer_b_kernel(tc, adj, ht, w, a_src, a_dst, b, offs, out
             queue.dma_start(ht_sb[:, a : a + 2, :], ht_view[:, a : a + 2, :])
         adj_sb = [held.tile([P, GRAPH], F32, name="adj%d" % ib) for ib in range(NB)]
         for ib in range(NB):
-            queue = nc.sync if ib % 2 == 0 else nc.scalar
-            queue.dma_start(adj_sb[ib][:], adj[ib * P : (ib + 1) * P, :])
+            nc.sync.dma_start(adj_sb[ib][:], adj[ib * P : (ib + 1) * P, :])
 
         ident_bf = held.tile([P, P], BF16, name="ident_bf")
-        ident_f32 = held.tile([P, P], F32, name="ident_f32")
         make_identity(nc, ident_bf[:])
-        make_identity(nc, ident_f32[:])
         ones_bf = held.tile([P, P], BF16, name="ones_bf")
         nc.vector.memset(ones_bf[:], 1.0)
         b_bf = held.tile([P, HEADS * DH], BF16, name="b_bf")
@@ -75,12 +77,12 @@ def tile_graphattentionlayer_b_kernel(tc, adj, ht, w, a_src, a_dst, b, offs, out
         nc.vector.tensor_copy(a_bf[:, :, 0:1], a_src_sb[:].unsqueeze(2))
         nc.vector.tensor_copy(a_bf[:, :, 1:2], a_dst_sb[:].unsqueeze(2))
 
-        wa_ps = ps_small.tile([P, FB, 2 * HEADS], F32, tag="small", name="wa_ps")
+        wa_ps = ps_acc.tile([P, FB, 2 * HEADS], F32, tag="acc", name="wa_ps")
         for a in range(FB):
             wt_ps = ps_flip.tile([P, QB, P], BF16, tag="flip", name="wt_ps")
             for qb in range(QB):
                 nc.tensor.transpose(wt_ps[:, qb, :], w_sb[:, a, qb * P : (qb + 1) * P], ident_bf[:])
-            wt_sb = pt_pool.tile([P, QB, P], BF16, tag="flipped", name="wt_sb")
+            wt_sb = ring.tile([P, QB, P], BF16, tag="flipped", name="wt_sb")
             nc.vector.tensor_copy(wt_sb[:], wt_ps[:])
             for qb in range(QB):
                 k = qb // 2
@@ -91,7 +93,7 @@ def tile_graphattentionlayer_b_kernel(tc, adj, ht, w, a_src, a_dst, b, offs, out
         wa_bf = held.tile([P, FB, 2 * HEADS], BF16, name="wa_bf")
         nc.vector.tensor_copy(wa_bf[:], wa_ps[:])
 
-        s_ps = ps_small.tile([P, NB, 2 * HEADS], F32, tag="small", name="s_ps")
+        s_ps = ps_acc.tile([P, NB, 2 * HEADS], F32, tag="acc", name="s_ps")
         for nb in range(NB):
             for a in range(FB):
                 nc.tensor.matmul(
@@ -106,74 +108,111 @@ def tile_graphattentionlayer_b_kernel(tc, adj, ht, w, a_src, a_dst, b, offs, out
         nc.scalar.activation(h1[:], s_view[:, :, :, 0], ACT.Exp, scale=0.8)
         nc.scalar.activation(g2[:], s_view[:, :, :, 1], ACT.Exp, scale=0.2)
 
-        h2 = held.tile([P, HEADS, NODES], F32, name="h2")
-        hwx = held.tile([P, NB, HEADS, ROW], BF16, name="hwx")
-        nc.scalar.copy(hwx[:, :, :, DH : DH + 1], g2[:].unsqueeze(3))
+        h2_terms = held.tile([P, TERMS, NB, HEADS], BF16, name="h2_terms")
+        left = h2_col
+        for term in range(TERMS):
+            nc.vector.tensor_copy(h2_terms[:, term], left[:])
+            if term + 1 < TERMS:
+                rest = held.tile([P, NB, HEADS], F32, name="rest%d" % term)
+                nc.vector.tensor_tensor(rest[:], left[:], h2_terms[:, term], ALU.subtract)
+                left = rest
+
+        h2 = [held.tile([P, NODES], F32, name="h2_%d" % k) for k in range(HEADS)]
+        hwx = [held.tile([P, NB, ROW], BF16, name="hwx_%d" % k) for k in range(HEADS)]
+        for k in range(HEADS):
+            nc.scalar.copy(hwx[k][:, :, DH : DH + 1], g2[:, :, k : k + 1])
 
         def spread_h2(k):
-            for half in range(NODES // HALF):
-                spread_ps = ps_wide.tile([P, HALF], F32, tag="wide", name="spread_ps")
-                for c in range(HALF // P):
-                    nb = half * (HALF // P) + c
-                    nc.tensor.matmul(
-                        spread_ps[:, c * P : (c + 1) * P],
-                        lhsT=h2_col[:, nb, k : k + 1].to_broadcast([P, P]), rhs=ident_f32[:],
-                        start=True, stop=True,
-                    )
-                nc.vector.tensor_copy(h2[:, k, half * HALF : (half + 1) * HALF], spread_ps[:])
+            for half in range(NODES // BANK):
+                spread_ps = ps_wide.tile([P, BANK], F32, tag="wide", name="spread_ps")
+                for c in range(BANK // P):
+                    nb = half * (BANK // P) + c
+                    for term in range(TERMS):
+                        nc.tensor.matmul(
+                            spread_ps[:, c * P : (c + 1) * P],
+                            lhsT=h2_terms[:, term, nb, k : k + 1].to_broadcast([P, P]), rhs=ident_bf[:],
+                            start=(term == 0), stop=(term == TERMS - 1),
+                        )
+                nc.scalar.copy(h2[k][:, half * BANK : (half + 1) * BANK], spread_ps[:])
 
-        def project(pair):
-            cols = slice(pair * HALF, (pair + 1) * HALF)
-            for nb in range(NB):
-                hw_ps = ps_wide.tile([P, HALF], F32, tag="wide", name="hw_ps")
-                for a in range(FB):
-                    nc.tensor.matmul(
-                        hw_ps[:], lhsT=ht_sb[:, a, nb * P : (nb + 1) * P], rhs=w_sb[:, a, cols],
-                        start=(a == 0), stop=False,
-                    )
-                nc.tensor.matmul(hw_ps[:], lhsT=ones_bf[:], rhs=b_bf[:, cols], start=False, stop=True)
-                for kk in range(2):
-                    k = 2 * pair + kk
-                    nc.scalar.activation(
-                        hwx[:, nb, k, 0:DH], hw_ps[:, kk * DH : (kk + 1) * DH], ACT.Copy,
-                        scale=g2[:, nb, k : k + 1],
-                    )
+        def project(k, nb):
+            cols = slice(k * DH, (k + 1) * DH)
+            hw_ps = ps_wide.tile([P, DH], F32, tag="wide", name="hw_ps")
+            for a in range(FB):
+                nc.tensor.matmul(
+                    hw_ps[:], lhsT=ht_sb[:, a, nb * P : (nb + 1) * P], rhs=w_sb[:, a, cols],
+                    start=(a == 0), stop=False,
+                )
+            nc.tensor.matmul(hw_ps[:], lhsT=ones_bf[:], rhs=b_bf[:, cols], start=False, stop=True)
+            nc.scalar.activation(hwx[k][:, nb, 0:DH], hw_ps[:], ACT.Copy, scale=g2[:, nb, k : k + 1])
 
-        def attend(ib, k, result):
+        products, rounded, flipped, sums, inverses, exps = {}, {}, {}, {}, {}, {}
+
+        def look_up(u):
+            k, ib = divmod(u, NB)
             e = e_pool.tile([P, NODES], F32, name="e")
             nc.vector.tensor_scalar(
-                e[:], h2[:, k, :], h1[:, ib, k : k + 1], 1.0, op0=ALU.mult, op1=ALU.max
+                e[:], h2[k][:], h1[:, ib, k : k + 1], 1.0, op0=ALU.mult, op1=ALU.max
             )
-            p = p_pool.tile([P, NODES], F32, name="p")
+            p = ring.tile([P, NODES], F32, name="p")
             nc.vector.tensor_tensor(p[:], adj_sb[ib][:].indirect(offsets[:]), e[:], ALU.mult)
-            p_bf = pb_pool.tile([P, NODES], BF16, name="p_bf")
-            nc.scalar.copy(p_bf[:], p[:])
+            products[u] = p
+
+        def round_p(u):
+            p_bf = ring.tile([P, NODES], BF16, name="p_bf")
+            nc.scalar.copy(p_bf[:], products.pop(u)[:])
+            rounded[u] = p_bf
+
+        def flip(u):
+            p_bf = rounded.pop(u)
             pt_ps = ps_flip.tile([P, NB, P], BF16, tag="flip", name="pt_ps")
             for jb in range(NB):
                 nc.tensor.transpose(pt_ps[:, jb, :], p_bf[:, jb * P : (jb + 1) * P], ident_bf[:])
-            pt = pt_pool.tile([P, NB, P], BF16, tag="flipped", name="pt")
+            pt = ring.tile([P, NB, P], BF16, tag="flipped", name="pt")
             nc.scalar.copy(pt[:], pt_ps[:])
-            acc = ps_acc.tile([P, DH + 1], F32, name="acc")
+            flipped[u] = pt
+
+        def weigh(u):
+            k = u // NB
+            pt = flipped.pop(u)
+            acc = ps_acc.tile([P, DH + 1], F32, tag="acc", name="acc")
             for jb in range(NB):
                 nc.tensor.matmul(
-                    acc[:], lhsT=pt[:, jb, :], rhs=hwx[:, jb, k, 0 : DH + 1],
+                    acc[:], lhsT=pt[:, jb, :], rhs=hwx[k][:, jb, 0 : DH + 1],
                     start=(jb == 0), stop=(jb == NB - 1),
                 )
             inv = tail.tile([P, 1], F32, name="inv")
             nc.vector.reciprocal(inv[:], acc[:, DH : DH + 1])
-            ex = tail.tile([P, DH], F32, name="ex")
-            nc.scalar.activation(ex[:], acc[:, 0:DH], ACT.Exp, scale=inv[:])
-            nc.vector.tensor_scalar(ex[:], ex[:], 1.0, -1.0, op0=ALU.min, op1=ALU.add)
-            nc.vector.scalar_tensor_tensor(
-                result, in0=acc[:, 0:DH], scalar=inv[:], in1=ex[:], op0=ALU.mult, op1=ALU.max
-            )
+            sums[u], inverses[u] = acc, inv
 
-        for pair in range(HEADS // 2):
-            spread_h2(2 * pair)
-            spread_h2(2 * pair + 1)
-            project(pair)
-            for ib in range(NB):
-                o = tail.tile([P, HALF], F32, name="o")
-                for kk in range(2):
-                    attend(ib, 2 * pair + kk, o[:, kk * DH : (kk + 1) * DH])
-                nc.sync.dma_start(out[ib * P : (ib + 1) * P, pair * HALF : (pair + 1) * HALF], o[:])
+        def exponent(u):
+            ex = tail.tile([P, DH], F32, name="ex")
+            nc.scalar.activation(ex[:], sums[u][:, 0:DH], ACT.Exp, scale=inverses[u][:])
+            exps[u] = ex
+
+        def elu_and_store(u):
+            k, ib = divmod(u, NB)
+            acc, inv, ex = sums.pop(u), inverses.pop(u), exps.pop(u)
+            nc.vector.tensor_scalar(ex[:], ex[:], 1.0, -1.0, op0=ALU.min, op1=ALU.add)
+            o = tail.tile([P, DH], F32, name="o")
+            nc.vector.scalar_tensor_tensor(
+                o[:], in0=acc[:, 0:DH], scalar=inv[:], in1=ex[:], op0=ALU.mult, op1=ALU.max
+            )
+            nc.sync.dma_start(out[ib * P : (ib + 1) * P, k * DH : (k + 1) * DH], o[:])
+
+        stages = (
+            (look_up, 0), (round_p, ROUND_LAG), (flip, FLIP_LAG), (weigh, WEIGH_LAG),
+            (exponent, EXP_LAG), (elu_and_store, ELU_LAG),
+        )
+        spread_h2(0)
+        for nb in range(NB):
+            project(0, nb)
+        for t in range(UNITS + ELU_LAG):
+            for stage, lag in stages:
+                if 0 <= t - lag < UNITS:
+                    stage(t - lag)
+            k, ib = divmod(t, NB)
+            if k + 1 < HEADS:
+                if ib == 0:
+                    spread_h2(k + 1)
+                project(k + 1, ib)

@@ -20,6 +20,7 @@ FLIP_LAG = 2
 WEIGH_LAG = 3
 EXP_LAG = 4
 ELU_LAG = 5
+PREPARE_LAG = 2
 
 FLOPS = 2 * FEATS * NODES * HEADS * DH + 2 * HEADS * NODES * NODES * DH
 
@@ -57,11 +58,9 @@ def tile_graphattentionlayer_b_kernel(tc, adj, ht, w, a_src, a_dst, b, offs, out
         w_view = w.rearrange("(p a) q -> p a q", a=FB)
         ht_view = ht.rearrange("(p a) n -> p a n", a=FB)
         for a in range(0, FB, 2):
-            queue = nc.sync if a % 4 == 0 else nc.scalar
-            queue.dma_start(w_sb[:, a : a + 2, :], w_view[:, a : a + 2, :])
+            nc.sync.dma_start(w_sb[:, a : a + 2, :], w_view[:, a : a + 2, :])
         for a in range(0, FB, 2):
-            queue = nc.sync if a % 4 == 0 else nc.scalar
-            queue.dma_start(ht_sb[:, a : a + 2, :], ht_view[:, a : a + 2, :])
+            nc.sync.dma_start(ht_sb[:, a : a + 2, :], ht_view[:, a : a + 2, :])
         adj_sb = [held.tile([P, GRAPH], F32, name="adj%d" % ib) for ib in range(NB)]
         for ib in range(NB):
             nc.sync.dma_start(adj_sb[ib][:], adj[ib * P : (ib + 1) * P, :])
@@ -93,6 +92,19 @@ def tile_graphattentionlayer_b_kernel(tc, adj, ht, w, a_src, a_dst, b, offs, out
         wa_bf = held.tile([P, FB, 2 * HEADS], BF16, name="wa_bf")
         nc.vector.tensor_copy(wa_bf[:], wa_ps[:])
 
+        h2 = [held.tile([P, NODES], F32, name="h2_%d" % k) for k in range(HEADS)]
+        hwx = [held.tile([P, NB, ROW], BF16, name="hwx_%d" % k) for k in range(HEADS)]
+
+        s2_ps = [ps_wide.tile([P, BANK], F32, tag="wide", name="s2_ps%d" % half) for half in range(NODES // BANK)]
+        for a in range(FB):
+            for half in range(NODES // BANK):
+                nc.tensor.matmul(
+                    s2_ps[half][:], lhsT=wa_bf[:, a, 1:2].to_broadcast([P, P]),
+                    rhs=ht_sb[:, a, half * BANK : (half + 1) * BANK], start=(a == 0), stop=(a == FB - 1),
+                )
+        for half in range(NODES // BANK):
+            nc.scalar.activation(h2[0][:, half * BANK : (half + 1) * BANK], s2_ps[half][:], ACT.Exp, scale=0.8)
+
         s_ps = ps_acc.tile([P, NB, 2 * HEADS], F32, tag="acc", name="s_ps")
         for nb in range(NB):
             for a in range(FB):
@@ -104,21 +116,19 @@ def tile_graphattentionlayer_b_kernel(tc, adj, ht, w, a_src, a_dst, b, offs, out
         h1 = held.tile([P, NB, HEADS], F32, name="h1")
         g2 = held.tile([P, NB, HEADS], F32, name="g2")
         h2_col = held.tile([P, NB, HEADS], F32, name="h2_col")
-        nc.scalar.activation(h2_col[:], s_view[:, :, :, 1], ACT.Exp, scale=0.8)
         nc.scalar.activation(h1[:], s_view[:, :, :, 0], ACT.Exp, scale=0.8)
         nc.scalar.activation(g2[:], s_view[:, :, :, 1], ACT.Exp, scale=0.2)
+        nc.scalar.activation(h2_col[:], s_view[:, :, :, 1], ACT.Exp, scale=0.8)
 
         h2_terms = held.tile([P, TERMS, NB, HEADS], BF16, name="h2_terms")
         left = h2_col
         for term in range(TERMS):
-            nc.vector.tensor_copy(h2_terms[:, term], left[:])
+            nc.gpsimd.tensor_copy(h2_terms[:, term], left[:])
             if term + 1 < TERMS:
                 rest = held.tile([P, NB, HEADS], F32, name="rest%d" % term)
-                nc.vector.tensor_tensor(rest[:], left[:], h2_terms[:, term], ALU.subtract)
+                nc.gpsimd.tensor_tensor(rest[:], left[:], h2_terms[:, term], ALU.subtract)
                 left = rest
 
-        h2 = [held.tile([P, NODES], F32, name="h2_%d" % k) for k in range(HEADS)]
-        hwx = [held.tile([P, NB, ROW], BF16, name="hwx_%d" % k) for k in range(HEADS)]
         for k in range(HEADS):
             nc.scalar.copy(hwx[k][:, :, DH : DH + 1], g2[:, :, k : k + 1])
 
@@ -204,15 +214,14 @@ def tile_graphattentionlayer_b_kernel(tc, adj, ht, w, a_src, a_dst, b, offs, out
             (look_up, 0), (round_p, ROUND_LAG), (flip, FLIP_LAG), (weigh, WEIGH_LAG),
             (exponent, EXP_LAG), (elu_and_store, ELU_LAG),
         )
-        spread_h2(0)
         for nb in range(NB):
             project(0, nb)
         for t in range(UNITS + ELU_LAG):
             for stage, lag in stages:
                 if 0 <= t - lag < UNITS:
                     stage(t - lag)
-            k, ib = divmod(t, NB)
-            if k + 1 < HEADS:
-                if ib == 0:
+            k, nb = divmod(t - PREPARE_LAG, NB)
+            if 0 <= k < HEADS - 1:
+                if nb == 0:
                     spread_h2(k + 1)
-                project(k + 1, ib)
+                project(k + 1, nb)

@@ -121,13 +121,15 @@ def tile_graphattentionlayer_b_kernel(tc, adj, ht, w, a_src, a_dst, b, offs, out
         nc.scalar.activation(h2_col[:], s_view[:, :, :, 1], ACT.Exp, scale=0.8)
 
         h2_terms = held.tile([P, TERMS, NB, HEADS], BF16, name="h2_terms")
-        left = h2_col
-        for term in range(TERMS):
-            nc.gpsimd.tensor_copy(h2_terms[:, term], left[:])
-            if term + 1 < TERMS:
-                rest = held.tile([P, NB, HEADS], F32, name="rest%d" % term)
-                nc.gpsimd.tensor_tensor(rest[:], left[:], h2_terms[:, term], ALU.subtract)
-                left = rest
+
+        def split_h2_col():
+            left = h2_col
+            for term in range(TERMS):
+                nc.vector.tensor_copy(h2_terms[:, term], left[:])
+                if term + 1 < TERMS:
+                    rest = held.tile([P, NB, HEADS], F32, name="rest%d" % term)
+                    nc.vector.tensor_tensor(rest[:], left[:], h2_terms[:, term], ALU.subtract)
+                    left = rest
 
         for k in range(HEADS):
             nc.scalar.copy(hwx[k][:, :, DH : DH + 1], g2[:, :, k : k + 1])
@@ -220,6 +222,8 @@ def tile_graphattentionlayer_b_kernel(tc, adj, ht, w, a_src, a_dst, b, offs, out
             for stage, lag in stages:
                 if 0 <= t - lag < UNITS:
                     stage(t - lag)
+            if t == PREPARE_LAG:
+                split_h2_col()
             k, nb = divmod(t - PREPARE_LAG, NB)
             if 0 <= k < HEADS - 1:
                 if nb == 0:

@@ -19,7 +19,7 @@ ROUND_LAG = 1
 FLIP_LAG = 2
 WEIGH_LAG = 3
 EXP_LAG = 4
-ELU_LAG = 5
+ELU_LAG = 24
 PREPARE_LAG = 2
 
 FLOPS = 2 * FEATS * NODES * HEADS * DH + 2 * HEADS * NODES * NODES * DH
@@ -39,8 +39,9 @@ def tile_graphattentionlayer_b_kernel(tc, adj, ht, w, a_src, a_dst, b, offs, out
         tc.tile_pool(name="e_pool", bufs=2) as e_pool,
         tc.tile_pool(name="ring", bufs=3) as ring,
         tc.tile_pool(name="tail", bufs=4) as tail,
+        tc.tile_pool(name="waiting", bufs=ELU_LAG - EXP_LAG + 2) as waiting,
         tc.psum_pool(name="ps_flip", bufs=3) as ps_flip,
-        tc.psum_pool(name="ps_acc", bufs=ELU_LAG - WEIGH_LAG + 1) as ps_acc,
+        tc.psum_pool(name="ps_acc", bufs=3) as ps_acc,
         tc.psum_pool(name="ps_wide", bufs=2) as ps_wide,
     ):
         offsets = lists.tile([P, NODES // 16], U16, name="offsets")
@@ -158,7 +159,7 @@ def tile_graphattentionlayer_b_kernel(tc, adj, ht, w, a_src, a_dst, b, offs, out
             nc.tensor.matmul(hw_ps[:], lhsT=ones_bf[:], rhs=b_bf[:, cols], start=False, stop=True)
             nc.scalar.activation(hwx[k][:, nb, 0:DH], hw_ps[:], ACT.Copy, scale=g2[:, nb, k : k + 1])
 
-        products, rounded, flipped, sums, inverses, exps = {}, {}, {}, {}, {}, {}
+        products, rounded, flipped, sums, inverses, halves = {}, {}, {}, {}, {}, {}
 
         def look_up(u):
             k, ib = divmod(u, NB)
@@ -197,24 +198,24 @@ def tile_graphattentionlayer_b_kernel(tc, adj, ht, w, a_src, a_dst, b, offs, out
             nc.vector.reciprocal(inv[:], acc[:, DH : DH + 1])
             sums[u], inverses[u] = acc, inv
 
-        def exponent(u):
-            ex = tail.tile([P, DH], F32, name="ex")
-            nc.scalar.activation(ex[:], sums[u][:, 0:DH], ACT.Exp, scale=inverses[u][:])
-            exps[u] = ex
+        def exp_and_relu(u):
+            acc, inv = sums.pop(u), inverses.pop(u)
+            ex = waiting.tile([P, DH], F32, name="ex")
+            nc.scalar.activation(ex[:], acc[:, 0:DH], ACT.Exp, scale=inv[:])
+            pos = waiting.tile([P, DH], F32, name="pos")
+            nc.scalar.activation(pos[:], acc[:, 0:DH], ACT.Relu, scale=inv[:])
+            halves[u] = (ex, pos)
 
         def elu_and_store(u):
             k, ib = divmod(u, NB)
-            acc, inv, ex = sums.pop(u), inverses.pop(u), exps.pop(u)
-            nc.vector.tensor_scalar(ex[:], ex[:], 1.0, -1.0, op0=ALU.min, op1=ALU.add)
+            ex, pos = halves.pop(u)
             o = tail.tile([P, DH], F32, name="o")
-            nc.vector.scalar_tensor_tensor(
-                o[:], in0=acc[:, 0:DH], scalar=inv[:], in1=ex[:], op0=ALU.mult, op1=ALU.max
-            )
+            nc.vector.scalar_tensor_tensor(o[:], in0=ex[:], scalar=-1.0, in1=pos[:], op0=ALU.add, op1=ALU.min)
             nc.sync.dma_start(out[ib * P : (ib + 1) * P, k * DH : (k + 1) * DH], o[:])
 
         stages = (
             (look_up, 0), (round_p, ROUND_LAG), (flip, FLIP_LAG), (weigh, WEIGH_LAG),
-            (exponent, EXP_LAG), (elu_and_store, ELU_LAG),
+            (exp_and_relu, EXP_LAG), (elu_and_store, ELU_LAG),
         )
         for nb in range(NB):
             project(0, nb)

@@ -77,25 +77,47 @@ def tile_graphattentionlayer_b_kernel(tc, adj, ht, w, a_src, a_dst, b, offs, out
         nc.vector.tensor_copy(a_bf[:, :, 0:1], a_src_sb[:].unsqueeze(2))
         nc.vector.tensor_copy(a_bf[:, :, 1:2], a_dst_sb[:].unsqueeze(2))
 
-        wa_ps = ps_acc.tile([P, FB, 2 * HEADS], F32, tag="acc", name="wa_ps")
-        for a in range(FB):
-            wt_ps = ps_flip.tile([P, QB, P], BF16, tag="flip", name="wt_ps")
-            for qb in range(QB):
-                nc.tensor.transpose(wt_ps[:, qb, :], w_sb[:, a, qb * P : (qb + 1) * P], ident_bf[:])
-            wt_sb = ring.tile([P, QB, P], BF16, tag="flipped", name="wt_sb")
-            nc.vector.tensor_copy(wt_sb[:], wt_ps[:])
-            for qb in range(QB):
-                k = qb // 2
-                nc.tensor.matmul(
-                    wa_ps[:, a, 2 * k : 2 * k + 2], lhsT=wt_sb[:, qb, :], rhs=a_bf[:, qb, :],
-                    start=(qb % 2 == 0), stop=(qb % 2 == 1),
-                )
-        wa_bf = held.tile([P, FB, 2 * HEADS], BF16, name="wa_bf")
-        nc.vector.tensor_copy(wa_bf[:], wa_ps[:])
-
         h2 = [held.tile([P, NODES], F32, name="h2_%d" % k) for k in range(HEADS)]
         hwx = [held.tile([P, NB, ROW], BF16, name="hwx_%d" % k) for k in range(HEADS)]
+        wa_bf = held.tile([P, FB, 2 * HEADS], BF16, name="wa_bf")
+        h1 = held.tile([P, NB, HEADS], F32, name="h1")
+        g2 = held.tile([P, NB, HEADS], F32, name="g2")
+        h2_col = held.tile([P, NB, HEADS], F32, name="h2_col")
 
+        def score_weights(k):
+            wa_ps = ps_acc.tile([P, FB, 2], F32, tag="acc", name="wa_ps")
+            for first in range(0, FB, FB // 2):
+                wt_ps = ps_flip.tile([P, FB // 2, 2, P], BF16, tag="flip", name="wt_ps")
+                for a in range(FB // 2):
+                    for c in range(2):
+                        qb = 2 * k + c
+                        nc.tensor.transpose(wt_ps[:, a, c, :], w_sb[:, first + a, qb * P : (qb + 1) * P], ident_bf[:])
+                wt_sb = ring.tile([P, FB // 2, 2, P], BF16, tag="flipped", name="wt_sb")
+                nc.vector.tensor_copy(wt_sb[:], wt_ps[:])
+                for a in range(FB // 2):
+                    for c in range(2):
+                        nc.tensor.matmul(
+                            wa_ps[:, first + a, :], lhsT=wt_sb[:, a, c, :], rhs=a_bf[:, 2 * k + c, :],
+                            start=(c == 0), stop=(c == 1),
+                        )
+            nc.vector.tensor_copy(wa_bf[:, :, 2 * k : 2 * k + 2], wa_ps[:])
+
+        def scores(k0, k1):
+            s_ps = ps_acc.tile([P, NB, 2 * (k1 - k0)], F32, tag="acc", name="s_ps")
+            for nb in range(NB):
+                for a in range(FB):
+                    nc.tensor.matmul(
+                        s_ps[:, nb, :], lhsT=ht_sb[:, a, nb * P : (nb + 1) * P], rhs=wa_bf[:, a, 2 * k0 : 2 * k1],
+                        start=(a == 0), stop=(a == FB - 1),
+                    )
+            s_view = s_ps[:].rearrange("p n (k t) -> p n k t", t=2)
+            nc.scalar.activation(h1[:, :, k0:k1], s_view[:, :, :, 0], ACT.Exp, scale=0.8)
+            nc.scalar.activation(g2[:, :, k0:k1], s_view[:, :, :, 1], ACT.Exp, scale=0.2)
+            nc.scalar.activation(h2_col[:, :, k0:k1], s_view[:, :, :, 1], ACT.Exp, scale=0.8)
+            for k in range(k0, k1):
+                nc.scalar.copy(hwx[k][:, :, DH : DH + 1], g2[:, :, k : k + 1])
+
+        score_weights(0)
         s2_ps = [ps_wide.tile([P, BANK], F32, tag="wide", name="s2_ps%d" % half) for half in range(NODES // BANK)]
         for a in range(FB):
             for half in range(NODES // BANK):
@@ -105,21 +127,10 @@ def tile_graphattentionlayer_b_kernel(tc, adj, ht, w, a_src, a_dst, b, offs, out
                 )
         for half in range(NODES // BANK):
             nc.scalar.activation(h2[0][:, half * BANK : (half + 1) * BANK], s2_ps[half][:], ACT.Exp, scale=0.8)
-
-        s_ps = ps_acc.tile([P, NB, 2 * HEADS], F32, tag="acc", name="s_ps")
-        for nb in range(NB):
-            for a in range(FB):
-                nc.tensor.matmul(
-                    s_ps[:, nb, :], lhsT=ht_sb[:, a, nb * P : (nb + 1) * P], rhs=wa_bf[:, a, :],
-                    start=(a == 0), stop=(a == FB - 1),
-                )
-        s_view = s_ps[:].rearrange("p n (k t) -> p n k t", t=2)
-        h1 = held.tile([P, NB, HEADS], F32, name="h1")
-        g2 = held.tile([P, NB, HEADS], F32, name="g2")
-        h2_col = held.tile([P, NB, HEADS], F32, name="h2_col")
-        nc.scalar.activation(h1[:], s_view[:, :, :, 0], ACT.Exp, scale=0.8)
-        nc.scalar.activation(g2[:], s_view[:, :, :, 1], ACT.Exp, scale=0.2)
-        nc.scalar.activation(h2_col[:], s_view[:, :, :, 1], ACT.Exp, scale=0.8)
+        scores(0, 1)
+        for k in range(1, HEADS):
+            score_weights(k)
+        scores(1, HEADS)
 
         h2_terms = held.tile([P, TERMS, NB, HEADS], BF16, name="h2_terms")
 
@@ -131,9 +142,6 @@ def tile_graphattentionlayer_b_kernel(tc, adj, ht, w, a_src, a_dst, b, offs, out
                     rest = held.tile([P, NB, HEADS], F32, name="rest%d" % term)
                     nc.vector.tensor_tensor(rest[:], left[:], h2_terms[:, term], ALU.subtract)
                     left = rest
-
-        for k in range(HEADS):
-            nc.scalar.copy(hwx[k][:, :, DH : DH + 1], g2[:, :, k : k + 1])
 
         def spread_h2(k):
             for half in range(NODES // BANK):

@@ -41,8 +41,8 @@ def tile_graphattentionlayer_b_kernel(tc, adj, ht, w, a_src, a_dst, b, offs, out
         tc.tile_pool(name="tail", bufs=4) as tail,
         tc.tile_pool(name="waiting", bufs=ELU_LAG - EXP_LAG + 2) as waiting,
         tc.psum_pool(name="ps_flip", bufs=3) as ps_flip,
-        tc.psum_pool(name="ps_acc", bufs=3) as ps_acc,
-        tc.psum_pool(name="ps_wide", bufs=2) as ps_wide,
+        tc.psum_pool(name="ps_acc", bufs=2) as ps_acc,
+        tc.psum_pool(name="ps_wide", bufs=3) as ps_wide,
     ):
         offsets = lists.tile([P, NODES // 16], U16, name="offsets")
         nc.sync.dma_start(offsets[:], offs)

@@ -14,6 +14,7 @@ BANK = 512
 ROW = DH + 2
 UNITS = HEADS * NB
 TERMS = 3
+A_ROWS = 64
 
 ROUND_LAG = 1
 FLIP_LAG = 2
@@ -45,26 +46,36 @@ def tile_graphattentionlayer_b_kernel(tc, adj, ht, w, a_src, a_dst, b, offs, out
         tc.psum_pool(name="ps_wide", bufs=3) as ps_wide,
     ):
         offsets = lists.tile([P, NODES // 16], U16, name="offsets")
-        nc.sync.dma_start(offsets[:], offs)
 
-        a_src_sb = held.tile([P, QB], F32, name="a_src_sb")
-        a_dst_sb = held.tile([P, QB], F32, name="a_dst_sb")
+        a_rows = held.tile([A_ROWS, P], F32, name="a_rows")
+        nc.vector.memset(a_rows[:], 0.0)
         b_row = held.tile([1, HEADS * DH], F32, name="b_row")
-        nc.scalar.dma_start(a_src_sb[:], a_src.rearrange("(a p) o -> p (a o)", p=P))
-        nc.scalar.dma_start(a_dst_sb[:], a_dst.rearrange("(a p) o -> p (a o)", p=P))
+        nc.scalar.dma_start(a_rows[0:QB, :], a_src.rearrange("(a p) o -> a (p o)", p=P))
+        nc.scalar.dma_start(a_rows[QB : 2 * QB, :], a_dst.rearrange("(a p) o -> a (p o)", p=P))
         nc.scalar.dma_start(b_row[:], b.rearrange("q o -> o q"))
 
         w_sb = held.tile([P, FB, HEADS * DH], BF16, name="w_sb")
         ht_sb = held.tile([P, FB, NODES], BF16, name="ht_sb")
         w_view = w.rearrange("(p a) q -> p a q", a=FB)
         ht_view = ht.rearrange("(p a) n -> p a n", a=FB)
-        for a in range(0, FB, 2):
-            nc.sync.dma_start(w_sb[:, a : a + 2, :], w_view[:, a : a + 2, :])
+        adj_sb = [held.tile([P, GRAPH], F32, name="adj%d" % ib) for ib in range(NB)]
+
+        def load_w(k):
+            cols = slice(k * DH, (k + 1) * DH)
+            nc.sync.dma_start(w_sb[:, :, cols], w_view[:, :, cols])
+
+        def load_adj(ib):
+            nc.sync.dma_start(adj_sb[ib][:], adj[ib * P : (ib + 1) * P, :])
+
+        load_w(0)
         for a in range(0, FB, 2):
             nc.sync.dma_start(ht_sb[:, a : a + 2, :], ht_view[:, a : a + 2, :])
-        adj_sb = [held.tile([P, GRAPH], F32, name="adj%d" % ib) for ib in range(NB)]
-        for ib in range(NB):
-            nc.sync.dma_start(adj_sb[ib][:], adj[ib * P : (ib + 1) * P, :])
+        nc.sync.dma_start(offsets[:], offs)
+        load_adj(0)
+        for k in range(1, HEADS):
+            load_w(k)
+        for ib in range(1, NB):
+            load_adj(ib)
 
         ident_bf = held.tile([P, P], BF16, name="ident_bf")
         make_identity(nc, ident_bf[:])
@@ -73,9 +84,12 @@ def tile_graphattentionlayer_b_kernel(tc, adj, ht, w, a_src, a_dst, b, offs, out
         b_bf = held.tile([P, HEADS * DH], BF16, name="b_bf")
         nc.gpsimd.memset(b_bf[:], 0.0)
         nc.vector.tensor_copy(b_bf[0:1, :], b_row[:])
+        ident_a = held.tile([A_ROWS, A_ROWS], F32, name="ident_a")
+        make_identity(nc, ident_a[:])
+        a_ps = ps_acc.tile([P, A_ROWS], F32, tag="acc", name="a_ps")
+        nc.tensor.transpose(a_ps[:], a_rows[:], ident_a[:])
         a_bf = held.tile([P, QB, 2], BF16, name="a_bf")
-        nc.vector.tensor_copy(a_bf[:, :, 0:1], a_src_sb[:].unsqueeze(2))
-        nc.vector.tensor_copy(a_bf[:, :, 1:2], a_dst_sb[:].unsqueeze(2))
+        nc.vector.tensor_copy(a_bf[:], a_ps[:, 0 : 2 * QB].rearrange("p (t a) -> p a t", t=2))
 
         h2 = [held.tile([P, NODES], F32, name="h2_%d" % k) for k in range(HEADS)]
         hwx = [held.tile([P, NB, ROW], BF16, name="hwx_%d" % k) for k in range(HEADS)]
@@ -85,6 +99,7 @@ def tile_graphattentionlayer_b_kernel(tc, adj, ht, w, a_src, a_dst, b, offs, out
         h2_col = held.tile([P, NB, HEADS], F32, name="h2_col")
 
         def score_weights(k):
+            copy_out = nc.vector.tensor_copy if k == 0 else nc.scalar.copy
             wa_ps = ps_acc.tile([P, FB, 2], F32, tag="acc", name="wa_ps")
             for first in range(0, FB, FB // 2):
                 wt_ps = ps_flip.tile([P, FB // 2, 2, P], BF16, tag="flip", name="wt_ps")
@@ -93,14 +108,14 @@ def tile_graphattentionlayer_b_kernel(tc, adj, ht, w, a_src, a_dst, b, offs, out
                         qb = 2 * k + c
                         nc.tensor.transpose(wt_ps[:, a, c, :], w_sb[:, first + a, qb * P : (qb + 1) * P], ident_bf[:])
                 wt_sb = ring.tile([P, FB // 2, 2, P], BF16, tag="flipped", name="wt_sb")
-                nc.vector.tensor_copy(wt_sb[:], wt_ps[:])
+                copy_out(wt_sb[:], wt_ps[:])
                 for a in range(FB // 2):
                     for c in range(2):
                         nc.tensor.matmul(
                             wa_ps[:, first + a, :], lhsT=wt_sb[:, a, c, :], rhs=a_bf[:, 2 * k + c, :],
                             start=(c == 0), stop=(c == 1),
                         )
-            nc.vector.tensor_copy(wa_bf[:, :, 2 * k : 2 * k + 2], wa_ps[:])
+            copy_out(wa_bf[:, :, 2 * k : 2 * k + 2], wa_ps[:])
 
         def scores(k0, k1):
             s_ps = ps_acc.tile([P, NB, 2 * (k1 - k0)], F32, tag="acc", name="s_ps")

@@ -50,9 +50,8 @@ def tile_graphattentionlayer_b_kernel(tc, adj, ht, w, a_src, a_dst, b, offs, out
         a_rows = held.tile([A_ROWS, P], F32, name="a_rows")
         nc.vector.memset(a_rows[:], 0.0)
         b_row = held.tile([1, HEADS * DH], F32, name="b_row")
-        nc.scalar.dma_start(a_rows[0:QB, :], a_src.rearrange("(a p) o -> a (p o)", p=P))
-        nc.scalar.dma_start(a_rows[QB : 2 * QB, :], a_dst.rearrange("(a p) o -> a (p o)", p=P))
-        nc.scalar.dma_start(b_row[:], b.rearrange("q o -> o q"))
+        nc.sync.dma_start(a_rows[0:QB, :], a_src.rearrange("(a p) o -> a (p o)", p=P))
+        nc.sync.dma_start(a_rows[QB : 2 * QB, :], a_dst.rearrange("(a p) o -> a (p o)", p=P))
 
         w_sb = held.tile([P, FB, HEADS * DH], BF16, name="w_sb")
         ht_sb = held.tile([P, FB, NODES], BF16, name="ht_sb")
@@ -71,6 +70,7 @@ def tile_graphattentionlayer_b_kernel(tc, adj, ht, w, a_src, a_dst, b, offs, out
         for a in range(0, FB, 2):
             nc.sync.dma_start(ht_sb[:, a : a + 2, :], ht_view[:, a : a + 2, :])
         nc.sync.dma_start(offsets[:], offs)
+        nc.sync.dma_start(b_row[:], b.rearrange("q o -> o q"))
         load_adj(0)
         for k in range(1, HEADS):
             load_w(k)
@@ -83,7 +83,7 @@ def tile_graphattentionlayer_b_kernel(tc, adj, ht, w, a_src, a_dst, b, offs, out
         nc.vector.memset(ones_bf[:], 1.0)
         b_bf = held.tile([P, HEADS * DH], BF16, name="b_bf")
         nc.gpsimd.memset(b_bf[:], 0.0)
-        nc.vector.tensor_copy(b_bf[0:1, :], b_row[:])
+        nc.scalar.copy(b_bf[0:1, :], b_row[:])
         ident_a = held.tile([A_ROWS, A_ROWS], F32, name="ident_a")
         make_identity(nc, ident_a[:])
         a_ps = ps_acc.tile([P, A_ROWS], F32, tag="acc", name="a_ps")
@@ -108,7 +108,10 @@ def tile_graphattentionlayer_b_kernel(tc, adj, ht, w, a_src, a_dst, b, offs, out
                         qb = 2 * k + c
                         nc.tensor.transpose(wt_ps[:, a, c, :], w_sb[:, first + a, qb * P : (qb + 1) * P], ident_bf[:])
                 wt_sb = ring.tile([P, FB // 2, 2, P], BF16, tag="flipped", name="wt_sb")
-                copy_out(wt_sb[:], wt_ps[:])
+                if first == 0:
+                    copy_out(wt_sb[:], wt_ps[:])
+                else:
+                    nc.scalar.copy(wt_sb[:], wt_ps[:])
                 for a in range(FB // 2):
                     for c in range(2):
                         nc.tensor.matmul(
@@ -117,35 +120,36 @@ def tile_graphattentionlayer_b_kernel(tc, adj, ht, w, a_src, a_dst, b, offs, out
                         )
             copy_out(wa_bf[:, :, 2 * k : 2 * k + 2], wa_ps[:])
 
-        def scores(k0, k1):
-            s_ps = ps_acc.tile([P, NB, 2 * (k1 - k0)], F32, tag="acc", name="s_ps")
-            for nb in range(NB):
+        def scores(k0, k1, n0, n1):
+            s_ps = ps_acc.tile([P, n1 - n0, 2 * (k1 - k0)], F32, tag="acc", name="s_ps")
+            for nb in range(n0, n1):
                 for a in range(FB):
                     nc.tensor.matmul(
-                        s_ps[:, nb, :], lhsT=ht_sb[:, a, nb * P : (nb + 1) * P], rhs=wa_bf[:, a, 2 * k0 : 2 * k1],
+                        s_ps[:, nb - n0, :], lhsT=ht_sb[:, a, nb * P : (nb + 1) * P], rhs=wa_bf[:, a, 2 * k0 : 2 * k1],
                         start=(a == 0), stop=(a == FB - 1),
                     )
             s_view = s_ps[:].rearrange("p n (k t) -> p n k t", t=2)
-            nc.scalar.activation(h1[:, :, k0:k1], s_view[:, :, :, 0], ACT.Exp, scale=0.8)
-            nc.scalar.activation(g2[:, :, k0:k1], s_view[:, :, :, 1], ACT.Exp, scale=0.2)
-            nc.scalar.activation(h2_col[:, :, k0:k1], s_view[:, :, :, 1], ACT.Exp, scale=0.8)
+            nc.scalar.activation(h1[:, n0:n1, k0:k1], s_view[:, :, :, 0], ACT.Exp, scale=0.8)
+            nc.scalar.activation(g2[:, n0:n1, k0:k1], s_view[:, :, :, 1], ACT.Exp, scale=0.2)
+            nc.scalar.activation(h2_col[:, n0:n1, k0:k1], s_view[:, :, :, 1], ACT.Exp, scale=0.8)
             for k in range(k0, k1):
-                nc.scalar.copy(hwx[k][:, :, DH : DH + 1], g2[:, :, k : k + 1])
+                nc.scalar.copy(hwx[k][:, n0:n1, DH : DH + 1], g2[:, n0:n1, k : k + 1])
 
         score_weights(0)
+        scores(0, 1, 0, 1)
         s2_ps = [ps_wide.tile([P, BANK], F32, tag="wide", name="s2_ps%d" % half) for half in range(NODES // BANK)]
-        for a in range(FB):
-            for half in range(NODES // BANK):
+        for half in range(NODES // BANK):
+            for a in range(FB):
                 nc.tensor.matmul(
                     s2_ps[half][:], lhsT=wa_bf[:, a, 1:2].to_broadcast([P, P]),
                     rhs=ht_sb[:, a, half * BANK : (half + 1) * BANK], start=(a == 0), stop=(a == FB - 1),
                 )
         for half in range(NODES // BANK):
             nc.scalar.activation(h2[0][:, half * BANK : (half + 1) * BANK], s2_ps[half][:], ACT.Exp, scale=0.8)
-        scores(0, 1)
+        scores(0, 1, 1, NB)
         for k in range(1, HEADS):
             score_weights(k)
-        scores(1, HEADS)
+        scores(1, HEADS, 0, NB)
 
         h2_terms = held.tile([P, TERMS, NB, HEADS], BF16, name="h2_terms")
 

@@ -13,7 +13,7 @@ QB = HEADS * DH // P
 BANK = 512
 ROW = DH + 2
 UNITS = HEADS * NB
-TERMS = 3
+H2_COLS = 32
 A_ROWS = 64
 
 ROUND_LAG = 1
@@ -84,6 +84,8 @@ def tile_graphattentionlayer_b_kernel(tc, adj, ht, w, a_src, a_dst, b, offs, out
         b_bf = held.tile([P, HEADS * DH], BF16, name="b_bf")
         nc.gpsimd.memset(b_bf[:], 0.0)
         nc.scalar.copy(b_bf[0:1, :], b_row[:])
+        ident_f = held.tile([P, P], F32, name="ident_f")
+        make_identity(nc, ident_f[:])
         ident_a = held.tile([A_ROWS, A_ROWS], F32, name="ident_a")
         make_identity(nc, ident_a[:])
         a_ps = ps_acc.tile([P, A_ROWS], F32, tag="acc", name="a_ps")
@@ -96,7 +98,8 @@ def tile_graphattentionlayer_b_kernel(tc, adj, ht, w, a_src, a_dst, b, offs, out
         wa_bf = held.tile([P, FB, 2 * HEADS], BF16, name="wa_bf")
         h1 = held.tile([P, NB, HEADS], F32, name="h1")
         g2 = held.tile([P, NB, HEADS], F32, name="g2")
-        h2_col = held.tile([P, NB, HEADS], F32, name="h2_col")
+        h2_col = held.tile([P, H2_COLS], F32, name="h2_col")
+        nc.vector.memset(h2_col[:], 0.0)
 
         def score_weights(k):
             copy_out = nc.vector.tensor_copy if k == 0 else nc.scalar.copy
@@ -131,8 +134,10 @@ def tile_graphattentionlayer_b_kernel(tc, adj, ht, w, a_src, a_dst, b, offs, out
             s_view = s_ps[:].rearrange("p n (k t) -> p n k t", t=2)
             nc.scalar.activation(h1[:, n0:n1, k0:k1], s_view[:, :, :, 0], ACT.Exp, scale=0.8)
             nc.scalar.activation(g2[:, n0:n1, k0:k1], s_view[:, :, :, 1], ACT.Exp, scale=0.2)
-            nc.scalar.activation(h2_col[:, n0:n1, k0:k1], s_view[:, :, :, 1], ACT.Exp, scale=0.8)
             for k in range(k0, k1):
+                if k > 0:
+                    cols = slice((k - 1) * NB + n0, (k - 1) * NB + n1)
+                    nc.scalar.activation(h2_col[:, cols], s_view[:, :, k - k0, 1], ACT.Exp, scale=0.8)
                 nc.scalar.copy(hwx[k][:, n0:n1, DH : DH + 1], g2[:, n0:n1, k : k + 1])
 
         score_weights(0)
@@ -151,29 +156,15 @@ def tile_graphattentionlayer_b_kernel(tc, adj, ht, w, a_src, a_dst, b, offs, out
             score_weights(k)
         scores(1, HEADS, 0, NB)
 
-        h2_terms = held.tile([P, TERMS, NB, HEADS], BF16, name="h2_terms")
-
-        def split_h2_col():
-            left = h2_col
-            for term in range(TERMS):
-                nc.vector.tensor_copy(h2_terms[:, term], left[:])
-                if term + 1 < TERMS:
-                    rest = held.tile([P, NB, HEADS], F32, name="rest%d" % term)
-                    nc.vector.tensor_tensor(rest[:], left[:], h2_terms[:, term], ALU.subtract)
-                    left = rest
-
-        def spread_h2(k):
-            for half in range(NODES // BANK):
-                spread_ps = ps_wide.tile([P, BANK], F32, tag="wide", name="spread_ps")
-                for c in range(BANK // P):
-                    nb = half * (BANK // P) + c
-                    for term in range(TERMS):
-                        nc.tensor.matmul(
-                            spread_ps[:, c * P : (c + 1) * P],
-                            lhsT=h2_terms[:, term, nb, k : k + 1].to_broadcast([P, P]), rhs=ident_bf[:],
-                            start=(term == 0), stop=(term == TERMS - 1),
-                        )
-                nc.scalar.copy(h2[k][:, half * BANK : (half + 1) * BANK], spread_ps[:])
+        h2_rows_ps = ps_acc.tile([H2_COLS, P], F32, tag="acc", name="h2_rows_ps")
+        nc.tensor.transpose(h2_rows_ps[:], h2_col[:], ident_f[:])
+        h2_rows = held.tile([H2_COLS, P], F32, name="h2_rows")
+        nc.scalar.copy(h2_rows[:], h2_rows_ps[:])
+        parked = out[NODES - (HEADS - 1) : NODES, :]
+        nc.sync.dma_start(parked.rearrange("k (n p) -> (k n) p", p=P), h2_rows[0 : (HEADS - 1) * NB, :])
+        for k in range(1, HEADS):
+            row = parked[k - 1 : k, :].rearrange("o n -> (o n)")
+            nc.sync.dma_start(h2[k][:], row.partition_broadcast(P))
 
         def project(k, nb):
             cols = slice(k * DH, (k + 1) * DH)
@@ -250,10 +241,6 @@ def tile_graphattentionlayer_b_kernel(tc, adj, ht, w, a_src, a_dst, b, offs, out
             for stage, lag in stages:
                 if 0 <= t - lag < UNITS:
                     stage(t - lag)
-            if t == PREPARE_LAG:
-                split_h2_col()
             k, nb = divmod(t - PREPARE_LAG, NB)
             if 0 <= k < HEADS - 1:
-                if nb == 0:
-                    spread_h2(k + 1)
                 project(k + 1, nb)

@@ -14,6 +14,7 @@ BANK = 512
 ROW = DH + 2
 UNITS = HEADS * NB
 H2_COLS = 32
+LAST_UNITS = 4
 A_ROWS = 64
 
 ROUND_LAG = 1
@@ -38,7 +39,9 @@ def tile_graphattentionlayer_b_kernel(tc, adj, ht, w, a_src, a_dst, b, offs, out
         tc.tile_pool(name="lists", bufs=1) as lists,
         tc.tile_pool(name="held", bufs=1) as held,
         tc.tile_pool(name="e_pool", bufs=2) as e_pool,
-        tc.tile_pool(name="ring", bufs=3) as ring,
+        tc.tile_pool(name="p_pool", bufs=4) as p_pool,
+        tc.tile_pool(name="rounded_pool", bufs=2) as rounded_pool,
+        tc.tile_pool(name="flipped_pool", bufs=3) as flipped_pool,
         tc.tile_pool(name="tail", bufs=4) as tail,
         tc.tile_pool(name="waiting", bufs=ELU_LAG - EXP_LAG + 2) as waiting,
         tc.psum_pool(name="ps_flip", bufs=3) as ps_flip,
@@ -110,7 +113,7 @@ def tile_graphattentionlayer_b_kernel(tc, adj, ht, w, a_src, a_dst, b, offs, out
                     for c in range(2):
                         qb = 2 * k + c
                         nc.tensor.transpose(wt_ps[:, a, c, :], w_sb[:, first + a, qb * P : (qb + 1) * P], ident_bf[:])
-                wt_sb = ring.tile([P, FB // 2, 2, P], BF16, tag="flipped", name="wt_sb")
+                wt_sb = flipped_pool.tile([P, FB // 2, 2, P], BF16, tag="flipped", name="wt_sb")
                 if first == 0:
                     copy_out(wt_sb[:], wt_ps[:])
                 else:
@@ -182,15 +185,19 @@ def tile_graphattentionlayer_b_kernel(tc, adj, ht, w, a_src, a_dst, b, offs, out
         def look_up(u):
             k, ib = divmod(u, NB)
             e = e_pool.tile([P, NODES], F32, name="e")
-            nc.vector.tensor_scalar(
-                e[:], h2[k][:], h1[:, ib, k : k + 1], 1.0, op0=ALU.mult, op1=ALU.max
-            )
-            p = ring.tile([P, NODES], F32, name="p")
-            nc.vector.tensor_tensor(p[:], adj_sb[ib][:].indirect(offsets[:]), e[:], ALU.mult)
+            p = p_pool.tile([P, NODES], F32, name="p")
+            pieces = 2 if u == 0 else 1
+            for c in range(pieces):
+                cols = slice(c * NODES // pieces, (c + 1) * NODES // pieces)
+                listed = slice(cols.start // 16, cols.stop // 16)
+                nc.vector.tensor_scalar(
+                    e[:, cols], h2[k][:, cols], h1[:, ib, k : k + 1], 1.0, op0=ALU.mult, op1=ALU.max
+                )
+                nc.vector.tensor_tensor(p[:, cols], adj_sb[ib][:].indirect(offsets[:, listed]), e[:, cols], ALU.mult)
             products[u] = p
 
         def round_p(u):
-            p_bf = ring.tile([P, NODES], BF16, name="p_bf")
+            p_bf = rounded_pool.tile([P, NODES], BF16, name="p_bf")
             nc.scalar.copy(p_bf[:], products.pop(u)[:])
             rounded[u] = p_bf
 
@@ -199,8 +206,11 @@ def tile_graphattentionlayer_b_kernel(tc, adj, ht, w, a_src, a_dst, b, offs, out
             pt_ps = ps_flip.tile([P, NB, P], BF16, tag="flip", name="pt_ps")
             for jb in range(NB):
                 nc.tensor.transpose(pt_ps[:, jb, :], p_bf[:, jb * P : (jb + 1) * P], ident_bf[:])
-            pt = ring.tile([P, NB, P], BF16, tag="flipped", name="pt")
-            nc.scalar.copy(pt[:], pt_ps[:])
+            pt = flipped_pool.tile([P, NB, P], BF16, tag="flipped", name="pt")
+            if u < UNITS - LAST_UNITS:
+                nc.scalar.copy(pt[:], pt_ps[:])
+            else:
+                nc.vector.tensor_copy(pt[:], pt_ps[:])
             flipped[u] = pt
 
         def weigh(u):
@@ -221,7 +231,10 @@ def tile_graphattentionlayer_b_kernel(tc, adj, ht, w, a_src, a_dst, b, offs, out
             ex = waiting.tile([P, DH], F32, name="ex")
             nc.scalar.activation(ex[:], acc[:, 0:DH], ACT.Exp, scale=inv[:])
             pos = waiting.tile([P, DH], F32, name="pos")
-            nc.scalar.activation(pos[:], acc[:, 0:DH], ACT.Relu, scale=inv[:])
+            if u < UNITS - LAST_UNITS:
+                nc.scalar.activation(pos[:], acc[:, 0:DH], ACT.Relu, scale=inv[:])
+            else:
+                nc.vector.tensor_scalar(pos[:], acc[:, 0:DH], inv[:], 0.0, op0=ALU.mult, op1=ALU.max)
             halves[u] = (ex, pos)
 
         def elu_and_store(u):

@@ -14,15 +14,18 @@ BANK = 512
 ROW = DH + 2
 UNITS = HEADS * NB
 H2_COLS = 32
-LAST_UNITS = 4
+W0_COLS = DH + 16
+LAST_UNITS = 3
+FIRST_BLOCKS = 2
+UNIT_BUFS = 6
 A_ROWS = 64
 
 ROUND_LAG = 1
 FLIP_LAG = 2
-WEIGH_LAG = 3
-EXP_LAG = 4
+WEIGH_LAG = 4
+EXP_LAG = 5
 ELU_LAG = 24
-PREPARE_LAG = 2
+PREPARE_LAG = 4
 
 FLOPS = 2 * FEATS * NODES * HEADS * DH + 2 * HEADS * NODES * NODES * DH
 
@@ -39,13 +42,13 @@ def tile_graphattentionlayer_b_kernel(tc, adj, ht, w, a_src, a_dst, b, offs, out
         tc.tile_pool(name="lists", bufs=1) as lists,
         tc.tile_pool(name="held", bufs=1) as held,
         tc.tile_pool(name="e_pool", bufs=2) as e_pool,
-        tc.tile_pool(name="p_pool", bufs=4) as p_pool,
+        tc.tile_pool(name="unit_pool", bufs=UNIT_BUFS) as unit_pool,
         tc.tile_pool(name="rounded_pool", bufs=2) as rounded_pool,
-        tc.tile_pool(name="flipped_pool", bufs=3) as flipped_pool,
+        tc.tile_pool(name="wt_pool", bufs=3) as wt_pool,
         tc.tile_pool(name="tail", bufs=4) as tail,
         tc.tile_pool(name="waiting", bufs=ELU_LAG - EXP_LAG + 2) as waiting,
-        tc.psum_pool(name="ps_flip", bufs=3) as ps_flip,
-        tc.psum_pool(name="ps_acc", bufs=2) as ps_acc,
+        tc.psum_pool(name="ps_flip", bufs=2) as ps_flip,
+        tc.psum_pool(name="ps_acc", bufs=3) as ps_acc,
         tc.psum_pool(name="ps_wide", bufs=3) as ps_wide,
     ):
         offsets = lists.tile([P, NODES // 16], U16, name="offsets")
@@ -56,15 +59,14 @@ def tile_graphattentionlayer_b_kernel(tc, adj, ht, w, a_src, a_dst, b, offs, out
         nc.sync.dma_start(a_rows[0:QB, :], a_src.rearrange("(a p) o -> a (p o)", p=P))
         nc.sync.dma_start(a_rows[QB : 2 * QB, :], a_dst.rearrange("(a p) o -> a (p o)", p=P))
 
-        w_sb = held.tile([P, FB, HEADS * DH], BF16, name="w_sb")
+        w_sb = [held.tile([P, FB, W0_COLS if k == 0 else DH], BF16, name="w%d_sb" % k) for k in range(HEADS)]
         ht_sb = held.tile([P, FB, NODES], BF16, name="ht_sb")
         w_view = w.rearrange("(p a) q -> p a q", a=FB)
         ht_view = ht.rearrange("(p a) n -> p a n", a=FB)
         adj_sb = [held.tile([P, GRAPH], F32, name="adj%d" % ib) for ib in range(NB)]
 
         def load_w(k):
-            cols = slice(k * DH, (k + 1) * DH)
-            nc.sync.dma_start(w_sb[:, :, cols], w_view[:, :, cols])
+            nc.sync.dma_start(w_sb[k][:, :, 0:DH], w_view[:, :, k * DH : (k + 1) * DH])
 
         def load_adj(ib):
             nc.sync.dma_start(adj_sb[ib][:], adj[ib * P : (ib + 1) * P, :])
@@ -84,9 +86,9 @@ def tile_graphattentionlayer_b_kernel(tc, adj, ht, w, a_src, a_dst, b, offs, out
         make_identity(nc, ident_bf[:])
         ones_bf = held.tile([P, P], BF16, name="ones_bf")
         nc.vector.memset(ones_bf[:], 1.0)
-        b_bf = held.tile([P, HEADS * DH], BF16, name="b_bf")
+        b_bf = held.tile([P, HEADS, DH + 2], BF16, name="b_bf")
         nc.gpsimd.memset(b_bf[:], 0.0)
-        nc.scalar.copy(b_bf[0:1, :], b_row[:])
+        nc.scalar.copy(b_bf[0:1, :, 0:DH], b_row[:].rearrange("o (k d) -> o k d", d=DH))
         ident_f = held.tile([P, P], F32, name="ident_f")
         make_identity(nc, ident_f[:])
         ident_a = held.tile([A_ROWS, A_ROWS], F32, name="ident_a")
@@ -98,7 +100,8 @@ def tile_graphattentionlayer_b_kernel(tc, adj, ht, w, a_src, a_dst, b, offs, out
 
         h2 = [held.tile([P, NODES], F32, name="h2_%d" % k) for k in range(HEADS)]
         hwx = [held.tile([P, NB, ROW], BF16, name="hwx_%d" % k) for k in range(HEADS)]
-        wa_bf = held.tile([P, FB, 2 * HEADS], BF16, name="wa_bf")
+        wa_0 = w_sb[0][:, :, DH : DH + 2]
+        wa_later = held.tile([P, FB, 2 * (HEADS - 1)], BF16, name="wa_later")
         h1 = held.tile([P, NB, HEADS], F32, name="h1")
         g2 = held.tile([P, NB, HEADS], F32, name="g2")
         h2_col = held.tile([P, H2_COLS], F32, name="h2_col")
@@ -111,9 +114,8 @@ def tile_graphattentionlayer_b_kernel(tc, adj, ht, w, a_src, a_dst, b, offs, out
                 wt_ps = ps_flip.tile([P, FB // 2, 2, P], BF16, tag="flip", name="wt_ps")
                 for a in range(FB // 2):
                     for c in range(2):
-                        qb = 2 * k + c
-                        nc.tensor.transpose(wt_ps[:, a, c, :], w_sb[:, first + a, qb * P : (qb + 1) * P], ident_bf[:])
-                wt_sb = flipped_pool.tile([P, FB // 2, 2, P], BF16, tag="flipped", name="wt_sb")
+                        nc.tensor.transpose(wt_ps[:, a, c, :], w_sb[k][:, first + a, c * P : (c + 1) * P], ident_bf[:])
+                wt_sb = wt_pool.tile([P, FB // 2, 2, P], BF16, name="wt_sb")
                 if first == 0:
                     copy_out(wt_sb[:], wt_ps[:])
                 else:
@@ -124,40 +126,60 @@ def tile_graphattentionlayer_b_kernel(tc, adj, ht, w, a_src, a_dst, b, offs, out
                             wa_ps[:, first + a, :], lhsT=wt_sb[:, a, c, :], rhs=a_bf[:, 2 * k + c, :],
                             start=(c == 0), stop=(c == 1),
                         )
-            copy_out(wa_bf[:, :, 2 * k : 2 * k + 2], wa_ps[:])
+            copy_out(wa_0 if k == 0 else wa_later[:, :, 2 * k - 2 : 2 * k], wa_ps[:])
 
-        def scores(k0, k1, n0, n1):
-            s_ps = ps_acc.tile([P, n1 - n0, 2 * (k1 - k0)], F32, tag="acc", name="s_ps")
+        def scores(n0, n1, wa):
+            heads = wa.shape[2] // 2
+            s_ps = ps_acc.tile([P, n1 - n0, heads, 2], F32, tag="acc", name="s_ps")
             for nb in range(n0, n1):
                 for a in range(FB):
                     nc.tensor.matmul(
-                        s_ps[:, nb - n0, :], lhsT=ht_sb[:, a, nb * P : (nb + 1) * P], rhs=wa_bf[:, a, 2 * k0 : 2 * k1],
+                        s_ps[:, nb - n0], lhsT=ht_sb[:, a, nb * P : (nb + 1) * P], rhs=wa[:, a, :],
                         start=(a == 0), stop=(a == FB - 1),
                     )
-            s_view = s_ps[:].rearrange("p n (k t) -> p n k t", t=2)
-            nc.scalar.activation(h1[:, n0:n1, k0:k1], s_view[:, :, :, 0], ACT.Exp, scale=0.8)
-            nc.scalar.activation(g2[:, n0:n1, k0:k1], s_view[:, :, :, 1], ACT.Exp, scale=0.2)
-            for k in range(k0, k1):
-                if k > 0:
-                    cols = slice((k - 1) * NB + n0, (k - 1) * NB + n1)
-                    nc.scalar.activation(h2_col[:, cols], s_view[:, :, k - k0, 1], ACT.Exp, scale=0.8)
-                nc.scalar.copy(hwx[k][:, n0:n1, DH : DH + 1], g2[:, n0:n1, k : k + 1])
+            return s_ps
+
+        def exps(n0, n1, k, s1, s2):
+            nc.scalar.activation(h1[:, n0:n1, k], s1, ACT.Exp, scale=0.8)
+            nc.scalar.activation(g2[:, n0:n1, k], s2, ACT.Exp, scale=0.2)
+            nc.scalar.copy(hwx[k][:, n0:n1, DH], g2[:, n0:n1, k])
 
         score_weights(0)
-        scores(0, 1, 0, 1)
+        s_ps = scores(0, FIRST_BLOCKS, wa_0)
+        exps(0, FIRST_BLOCKS, 0, s_ps[:, :, 0, 0], s_ps[:, :, 0, 1])
         s2_ps = [ps_wide.tile([P, BANK], F32, tag="wide", name="s2_ps%d" % half) for half in range(NODES // BANK)]
         for half in range(NODES // BANK):
             for a in range(FB):
                 nc.tensor.matmul(
-                    s2_ps[half][:], lhsT=wa_bf[:, a, 1:2].to_broadcast([P, P]),
+                    s2_ps[half][:], lhsT=wa_0[:, a, 1:2].to_broadcast([P, P]),
                     rhs=ht_sb[:, a, half * BANK : (half + 1) * BANK], start=(a == 0), stop=(a == FB - 1),
                 )
         for half in range(NODES // BANK):
             nc.scalar.activation(h2[0][:, half * BANK : (half + 1) * BANK], s2_ps[half][:], ACT.Exp, scale=0.8)
-        scores(0, 1, 1, NB)
+
+        def project(k, nb):
+            with_scores = k == 0 and nb >= FIRST_BLOCKS
+            cols = DH + 2 if with_scores else DH
+            hw_ps = ps_wide.tile([P, cols], F32, tag="wide", name="hw_ps")
+            for a in range(FB):
+                nc.tensor.matmul(
+                    hw_ps[:], lhsT=ht_sb[:, a, nb * P : (nb + 1) * P], rhs=w_sb[k][:, a, 0:cols],
+                    start=(a == 0), stop=False,
+                )
+            nc.tensor.matmul(hw_ps[:], lhsT=ones_bf[:], rhs=b_bf[:, k, 0:cols], start=False, stop=True)
+            if with_scores:
+                exps(nb, nb + 1, 0, hw_ps[:, DH : DH + 1], hw_ps[:, DH + 1 : DH + 2])
+            nc.scalar.activation(hwx[k][:, nb, 0:DH], hw_ps[:, 0:DH], ACT.Copy, scale=g2[:, nb, k : k + 1])
+
+        for k in range(HEADS):
+            if k > 0:
+                score_weights(k)
+            for nb in range(k * NB // HEADS, (k + 1) * NB // HEADS):
+                project(0, nb)
+        s_ps = scores(0, NB, wa_later)
         for k in range(1, HEADS):
-            score_weights(k)
-        scores(1, HEADS, 0, NB)
+            exps(0, NB, k, s_ps[:, :, k - 1, 0], s_ps[:, :, k - 1, 1])
+            nc.scalar.activation(h2_col[:, (k - 1) * NB : k * NB], s_ps[:, :, k - 1, 1], ACT.Exp, scale=0.8)
 
         h2_rows_ps = ps_acc.tile([H2_COLS, P], F32, tag="acc", name="h2_rows_ps")
         nc.tensor.transpose(h2_rows_ps[:], h2_col[:], ident_f[:])
@@ -169,23 +191,12 @@ def tile_graphattentionlayer_b_kernel(tc, adj, ht, w, a_src, a_dst, b, offs, out
             row = parked[k - 1 : k, :].rearrange("o n -> (o n)")
             nc.sync.dma_start(h2[k][:], row.partition_broadcast(P))
 
-        def project(k, nb):
-            cols = slice(k * DH, (k + 1) * DH)
-            hw_ps = ps_wide.tile([P, DH], F32, tag="wide", name="hw_ps")
-            for a in range(FB):
-                nc.tensor.matmul(
-                    hw_ps[:], lhsT=ht_sb[:, a, nb * P : (nb + 1) * P], rhs=w_sb[:, a, cols],
-                    start=(a == 0), stop=False,
-                )
-            nc.tensor.matmul(hw_ps[:], lhsT=ones_bf[:], rhs=b_bf[:, cols], start=False, stop=True)
-            nc.scalar.activation(hwx[k][:, nb, 0:DH], hw_ps[:], ACT.Copy, scale=g2[:, nb, k : k + 1])
-
-        products, rounded, flipped, sums, inverses, halves = {}, {}, {}, {}, {}, {}
+        unit_tiles, rounded, flipped, sums, inverses, halves = {}, {}, {}, {}, {}, {}
 
         def look_up(u):
             k, ib = divmod(u, NB)
             e = e_pool.tile([P, NODES], F32, name="e")
-            p = p_pool.tile([P, NODES], F32, name="p")
+            p = unit_pool.tile([P, NODES], F32, name="p")
             pieces = 2 if u == 0 else 1
             for c in range(pieces):
                 cols = slice(c * NODES // pieces, (c + 1) * NODES // pieces)
@@ -194,11 +205,11 @@ def tile_graphattentionlayer_b_kernel(tc, adj, ht, w, a_src, a_dst, b, offs, out
                     e[:, cols], h2[k][:, cols], h1[:, ib, k : k + 1], 1.0, op0=ALU.mult, op1=ALU.max
                 )
                 nc.vector.tensor_tensor(p[:, cols], adj_sb[ib][:].indirect(offsets[:, listed]), e[:, cols], ALU.mult)
-            products[u] = p
+            unit_tiles[u] = p
 
         def round_p(u):
             p_bf = rounded_pool.tile([P, NODES], BF16, name="p_bf")
-            nc.scalar.copy(p_bf[:], products.pop(u)[:])
+            nc.scalar.copy(p_bf[:], unit_tiles[u][:])
             rounded[u] = p_bf
 
         def flip(u):
@@ -206,11 +217,11 @@ def tile_graphattentionlayer_b_kernel(tc, adj, ht, w, a_src, a_dst, b, offs, out
             pt_ps = ps_flip.tile([P, NB, P], BF16, tag="flip", name="pt_ps")
             for jb in range(NB):
                 nc.tensor.transpose(pt_ps[:, jb, :], p_bf[:, jb * P : (jb + 1) * P], ident_bf[:])
-            pt = flipped_pool.tile([P, NB, P], BF16, tag="flipped", name="pt")
+            pt = unit_tiles.pop(u)[:].bitcast(BF16)[:, 0:NODES].rearrange("q (b i) -> q b i", i=P)
             if u < UNITS - LAST_UNITS:
-                nc.scalar.copy(pt[:], pt_ps[:])
+                nc.scalar.copy(pt, pt_ps[:])
             else:
-                nc.vector.tensor_copy(pt[:], pt_ps[:])
+                nc.vector.tensor_copy(pt, pt_ps[:])
             flipped[u] = pt
 
         def weigh(u):
@@ -244,16 +255,17 @@ def tile_graphattentionlayer_b_kernel(tc, adj, ht, w, a_src, a_dst, b, offs, out
             nc.vector.scalar_tensor_tensor(o[:], in0=ex[:], scalar=-1.0, in1=pos[:], op0=ALU.add, op1=ALU.min)
             nc.sync.dma_start(out[ib * P : (ib + 1) * P, k * DH : (k + 1) * DH], o[:])
 
-        stages = (
-            (look_up, 0), (round_p, ROUND_LAG), (flip, FLIP_LAG), (weigh, WEIGH_LAG),
-            (exp_and_relu, EXP_LAG), (elu_and_store, ELU_LAG),
-        )
-        for nb in range(NB):
-            project(0, nb)
+        def stage(of_unit, u):
+            if 0 <= u < UNITS:
+                of_unit(u)
+
         for t in range(UNITS + ELU_LAG):
-            for stage, lag in stages:
-                if 0 <= t - lag < UNITS:
-                    stage(t - lag)
             k, nb = divmod(t - PREPARE_LAG, NB)
             if 0 <= k < HEADS - 1:
                 project(k + 1, nb)
+            stage(look_up, t)
+            stage(weigh, t - WEIGH_LAG)
+            stage(round_p, t - ROUND_LAG)
+            stage(flip, t - FLIP_LAG)
+            stage(exp_and_relu, t - EXP_LAG)
+            stage(elu_and_store, t - ELU_LAG)

import concourse.mybir as mybir
from concourse.masks import make_identity

P = 128
NODES = 1024
GRAPH = 2048
FEATS = 1024
HEADS = 4
DH = 256
NB = NODES // P
FB = FEATS // P
QB = HEADS * DH // P
BANK = 512
ROW = DH + 2
UNITS = HEADS * NB
H2_COLS = 32
W0_COLS = DH + 16
LAST_UNITS = 3
FIRST_BLOCKS = 2
UNIT_BUFS = 6
A_ROWS = 64

ROUND_LAG = 1
FLIP_LAG = 2
WEIGH_LAG = 4
EXP_LAG = 5
ELU_LAG = 24
PREPARE_LAG = 4

FLOPS = 2 * FEATS * NODES * HEADS * DH + 2 * HEADS * NODES * NODES * DH

F32 = mybir.dt.float32
BF16 = mybir.dt.bfloat16
U16 = mybir.dt.uint16
ALU = mybir.AluOpType
ACT = mybir.ActivationFunctionType


def tile_graphattentionlayer_b_kernel(tc, adj, ht, w, a_src, a_dst, b, offs, out):
    nc = tc.nc
    with (
        tc.tile_pool(name="lists", bufs=1) as lists,
        tc.tile_pool(name="held", bufs=1) as held,
        tc.tile_pool(name="e_pool", bufs=2) as e_pool,
        tc.tile_pool(name="unit_pool", bufs=UNIT_BUFS) as unit_pool,
        tc.tile_pool(name="rounded_pool", bufs=2) as rounded_pool,
        tc.tile_pool(name="wt_pool", bufs=3) as wt_pool,
        tc.tile_pool(name="tail", bufs=4) as tail,
        tc.tile_pool(name="waiting", bufs=ELU_LAG - EXP_LAG + 2) as waiting,
        tc.psum_pool(name="ps_flip", bufs=2) as ps_flip,
        tc.psum_pool(name="ps_acc", bufs=3) as ps_acc,
        tc.psum_pool(name="ps_wide", bufs=3) as ps_wide,
    ):
        offsets = lists.tile([P, NODES // 16], U16, name="offsets")

        a_rows = held.tile([A_ROWS, P], F32, name="a_rows")
        nc.vector.memset(a_rows[:], 0.0)
        b_row = held.tile([1, HEADS * DH], F32, name="b_row")
        nc.sync.dma_start(a_rows[0:QB, :], a_src.rearrange("(a p) o -> a (p o)", p=P))
        nc.sync.dma_start(a_rows[QB : 2 * QB, :], a_dst.rearrange("(a p) o -> a (p o)", p=P))

        w_sb = [held.tile([P, FB, W0_COLS if k == 0 else DH], BF16, name="w%d_sb" % k) for k in range(HEADS)]
        ht_sb = held.tile([P, FB, NODES], BF16, name="ht_sb")
        w_view = w.rearrange("(p a) q -> p a q", a=FB)
        ht_view = ht.rearrange("(p a) n -> p a n", a=FB)
        adj_sb = [held.tile([P, GRAPH], F32, name="adj%d" % ib) for ib in range(NB)]

        def load_w(k):
            nc.sync.dma_start(w_sb[k][:, :, 0:DH], w_view[:, :, k * DH : (k + 1) * DH])

        def load_adj(ib):
            nc.sync.dma_start(adj_sb[ib][:], adj[ib * P : (ib + 1) * P, :])

        load_w(0)
        for a in range(0, FB, 2):
            nc.sync.dma_start(ht_sb[:, a : a + 2, :], ht_view[:, a : a + 2, :])
        nc.sync.dma_start(offsets[:], offs)
        nc.sync.dma_start(b_row[:], b.rearrange("q o -> o q"))
        load_adj(0)
        for k in range(1, HEADS):
            load_w(k)
        for ib in range(1, NB):
            load_adj(ib)

        ident_bf = held.tile([P, P], BF16, name="ident_bf")
        make_identity(nc, ident_bf[:])
        ones_bf = held.tile([P, P], BF16, name="ones_bf")
        nc.vector.memset(ones_bf[:], 1.0)
        b_bf = held.tile([P, HEADS, DH + 2], BF16, name="b_bf")
        nc.gpsimd.memset(b_bf[:], 0.0)
        nc.scalar.copy(b_bf[0:1, :, 0:DH], b_row[:].rearrange("o (k d) -> o k d", d=DH))
        ident_f = held.tile([P, P], F32, name="ident_f")
        make_identity(nc, ident_f[:])
        ident_a = held.tile([A_ROWS, A_ROWS], F32, name="ident_a")
        make_identity(nc, ident_a[:])
        a_ps = ps_acc.tile([P, A_ROWS], F32, tag="acc", name="a_ps")
        nc.tensor.transpose(a_ps[:], a_rows[:], ident_a[:])
        a_bf = held.tile([P, QB, 2], BF16, name="a_bf")
        nc.vector.tensor_copy(a_bf[:], a_ps[:, 0 : 2 * QB].rearrange("p (t a) -> p a t", t=2))

        h2 = [held.tile([P, NODES], F32, name="h2_%d" % k) for k in range(HEADS)]
        hwx = [held.tile([P, NB, ROW], BF16, name="hwx_%d" % k) for k in range(HEADS)]
        wa_0 = w_sb[0][:, :, DH : DH + 2]
        wa_later = held.tile([P, FB, 2 * (HEADS - 1)], BF16, name="wa_later")
        h1 = held.tile([P, NB, HEADS], F32, name="h1")
        g2 = held.tile([P, NB, HEADS], F32, name="g2")
        h2_col = held.tile([P, H2_COLS], F32, name="h2_col")
        nc.vector.memset(h2_col[:], 0.0)

        def score_weights(k):
            copy_out = nc.vector.tensor_copy if k == 0 else nc.scalar.copy
            wa_ps = ps_acc.tile([P, FB, 2], F32, tag="acc", name="wa_ps")
            for first in range(0, FB, FB // 2):
                wt_ps = ps_flip.tile([P, FB // 2, 2, P], BF16, tag="flip", name="wt_ps")
                for a in range(FB // 2):
                    for c in range(2):
                        nc.tensor.transpose(wt_ps[:, a, c, :], w_sb[k][:, first + a, c * P : (c + 1) * P], ident_bf[:])
                wt_sb = wt_pool.tile([P, FB // 2, 2, P], BF16, name="wt_sb")
                if first == 0:
                    copy_out(wt_sb[:], wt_ps[:])
                else:
                    nc.scalar.copy(wt_sb[:], wt_ps[:])
                for a in range(FB // 2):
                    for c in range(2):
                        nc.tensor.matmul(
                            wa_ps[:, first + a, :], lhsT=wt_sb[:, a, c, :], rhs=a_bf[:, 2 * k + c, :],
                            start=(c == 0), stop=(c == 1),
                        )
            copy_out(wa_0 if k == 0 else wa_later[:, :, 2 * k - 2 : 2 * k], wa_ps[:])

        def scores(n0, n1, wa):
            heads = wa.shape[2] // 2
            s_ps = ps_acc.tile([P, n1 - n0, heads, 2], F32, tag="acc", name="s_ps")
            for nb in range(n0, n1):
                for a in range(FB):
                    nc.tensor.matmul(
                        s_ps[:, nb - n0], lhsT=ht_sb[:, a, nb * P : (nb + 1) * P], rhs=wa[:, a, :],
                        start=(a == 0), stop=(a == FB - 1),
                    )
            return s_ps

        def exps(n0, n1, k, s1, s2):
            nc.scalar.activation(h1[:, n0:n1, k], s1, ACT.Exp, scale=0.8)
            nc.scalar.activation(g2[:, n0:n1, k], s2, ACT.Exp, scale=0.2)
            nc.scalar.copy(hwx[k][:, n0:n1, DH], g2[:, n0:n1, k])

        score_weights(0)
        s_ps = scores(0, FIRST_BLOCKS, wa_0)
        exps(0, FIRST_BLOCKS, 0, s_ps[:, :, 0, 0], s_ps[:, :, 0, 1])
        s2_ps = [ps_wide.tile([P, BANK], F32, tag="wide", name="s2_ps%d" % half) for half in range(NODES // BANK)]
        for half in range(NODES // BANK):
            for a in range(FB):
                nc.tensor.matmul(
                    s2_ps[half][:], lhsT=wa_0[:, a, 1:2].to_broadcast([P, P]),
                    rhs=ht_sb[:, a, half * BANK : (half + 1) * BANK], start=(a == 0), stop=(a == FB - 1),
                )
        for half in range(NODES // BANK):
            nc.scalar.activation(h2[0][:, half * BANK : (half + 1) * BANK], s2_ps[half][:], ACT.Exp, scale=0.8)

        def project(k, nb):
            with_scores = k == 0 and nb >= FIRST_BLOCKS
            cols = DH + 2 if with_scores else DH
            hw_ps = ps_wide.tile([P, cols], F32, tag="wide", name="hw_ps")
            for a in range(FB):
                nc.tensor.matmul(
                    hw_ps[:], lhsT=ht_sb[:, a, nb * P : (nb + 1) * P], rhs=w_sb[k][:, a, 0:cols],
                    start=(a == 0), stop=False,
                )
            nc.tensor.matmul(hw_ps[:], lhsT=ones_bf[:], rhs=b_bf[:, k, 0:cols], start=False, stop=True)
            if with_scores:
                exps(nb, nb + 1, 0, hw_ps[:, DH : DH + 1], hw_ps[:, DH + 1 : DH + 2])
            nc.scalar.activation(hwx[k][:, nb, 0:DH], hw_ps[:, 0:DH], ACT.Copy, scale=g2[:, nb, k : k + 1])

        for k in range(HEADS):
            if k > 0:
                score_weights(k)
            for nb in range(k * NB // HEADS, (k + 1) * NB // HEADS):
                project(0, nb)
        s_ps = scores(0, NB, wa_later)
        for k in range(1, HEADS):
            exps(0, NB, k, s_ps[:, :, k - 1, 0], s_ps[:, :, k - 1, 1])
            nc.scalar.activation(h2_col[:, (k - 1) * NB : k * NB], s_ps[:, :, k - 1, 1], ACT.Exp, scale=0.8)

        h2_rows_ps = ps_acc.tile([H2_COLS, P], F32, tag="acc", name="h2_rows_ps")
        nc.tensor.transpose(h2_rows_ps[:], h2_col[:], ident_f[:])
        h2_rows = held.tile([H2_COLS, P], F32, name="h2_rows")
        nc.scalar.copy(h2_rows[:], h2_rows_ps[:])
        parked = out[NODES - (HEADS - 1) : NODES, :]
        nc.sync.dma_start(parked.rearrange("k (n p) -> (k n) p", p=P), h2_rows[0 : (HEADS - 1) * NB, :])
        for k in range(1, HEADS):
            row = parked[k - 1 : k, :].rearrange("o n -> (o n)")
            nc.sync.dma_start(h2[k][:], row.partition_broadcast(P))

        unit_tiles, rounded, flipped, sums, inverses, halves = {}, {}, {}, {}, {}, {}

        def look_up(u):
            k, ib = divmod(u, NB)
            e = e_pool.tile([P, NODES], F32, name="e")
            p = unit_pool.tile([P, NODES], F32, name="p")
            pieces = 2 if u == 0 else 1
            for c in range(pieces):
                cols = slice(c * NODES // pieces, (c + 1) * NODES // pieces)
                listed = slice(cols.start // 16, cols.stop // 16)
                nc.vector.tensor_scalar(
                    e[:, cols], h2[k][:, cols], h1[:, ib, k : k + 1], 1.0, op0=ALU.mult, op1=ALU.max
                )
                nc.vector.tensor_tensor(p[:, cols], adj_sb[ib][:].indirect(offsets[:, listed]), e[:, cols], ALU.mult)
            unit_tiles[u] = p

        def round_p(u):
            p_bf = rounded_pool.tile([P, NODES], BF16, name="p_bf")
            nc.scalar.copy(p_bf[:], unit_tiles[u][:])
            rounded[u] = p_bf

        def flip(u):
            p_bf = rounded.pop(u)
            pt_ps = ps_flip.tile([P, NB, P], BF16, tag="flip", name="pt_ps")
            for jb in range(NB):
                nc.tensor.transpose(pt_ps[:, jb, :], p_bf[:, jb * P : (jb + 1) * P], ident_bf[:])
            pt = unit_tiles.pop(u)[:].bitcast(BF16)[:, 0:NODES].rearrange("q (b i) -> q b i", i=P)
            if u < UNITS - LAST_UNITS:
                nc.scalar.copy(pt, pt_ps[:])
            else:
                nc.vector.tensor_copy(pt, pt_ps[:])
            flipped[u] = pt

        def weigh(u):
            k = u // NB
            pt = flipped.pop(u)
            acc = ps_acc.tile([P, DH + 1], F32, tag="acc", name="acc")
            for jb in range(NB):
                nc.tensor.matmul(
                    acc[:], lhsT=pt[:, jb, :], rhs=hwx[k][:, jb, 0 : DH + 1],
                    start=(jb == 0), stop=(jb == NB - 1),
                )
            inv = tail.tile([P, 1], F32, name="inv")
            nc.vector.reciprocal(inv[:], acc[:, DH : DH + 1])
            sums[u], inverses[u] = acc, inv

        def exp_and_relu(u):
            acc, inv = sums.pop(u), inverses.pop(u)
            ex = waiting.tile([P, DH], F32, name="ex")
            nc.scalar.activation(ex[:], acc[:, 0:DH], ACT.Exp, scale=inv[:])
            pos = waiting.tile([P, DH], F32, name="pos")
            if u < UNITS - LAST_UNITS:
                nc.scalar.activation(pos[:], acc[:, 0:DH], ACT.Relu, scale=inv[:])
            else:
                nc.vector.tensor_scalar(pos[:], acc[:, 0:DH], inv[:], 0.0, op0=ALU.mult, op1=ALU.max)
            halves[u] = (ex, pos)

        def elu_and_store(u):
            k, ib = divmod(u, NB)
            ex, pos = halves.pop(u)
            o = tail.tile([P, DH], F32, name="o")
            nc.vector.scalar_tensor_tensor(o[:], in0=ex[:], scalar=-1.0, in1=pos[:], op0=ALU.add, op1=ALU.min)
            nc.sync.dma_start(out[ib * P : (ib + 1) * P, k * DH : (k + 1) * DH], o[:])

        def stage(of_unit, u):
            if 0 <= u < UNITS:
                of_unit(u)

        for t in range(UNITS + ELU_LAG):
            k, nb = divmod(t - PREPARE_LAG, NB)
            if 0 <= k < HEADS - 1:
                project(k + 1, nb)
            stage(look_up, t)
            stage(weigh, t - WEIGH_LAG)
            stage(round_p, t - ROUND_LAG)
            stage(flip, t - FLIP_LAG)
            stage(exp_and_relu, t - EXP_LAG)
            stage(elu_and_store, t - ELU_LAG)
